import numpy as np
import ml_dtypes


def mxq(x, axis, fmt="e4m3"):
    dtype, down = {"e4m3": (ml_dtypes.float8_e4m3fn, 7), "e5m2": (ml_dtypes.float8_e5m2, 14)}[fmt]
    v = np.moveaxis(np.asarray(x, np.float32).astype(ml_dtypes.bfloat16).astype(np.float64), axis, -1)
    blocks = v.reshape(v.shape[:-1] + (-1, 32))
    amax = np.abs(blocks).max(-1, keepdims=True)
    byte = np.maximum(np.where(amax > 0, np.frexp(amax)[1] - 1 + 127, 0) - down, 1)
    scale = np.exp2(byte - 127.0)
    codes = (blocks / scale).astype(np.float32).astype(dtype).astype(np.float64)
    return np.moveaxis((codes * scale).reshape(v.shape), -1, axis)


WIDE = False


def mx_kscale(k):
    if not WIDE:
        return np.ones(k)
    levels = np.array([10, -10, 5, -5, 0])
    a = np.random.permutation(np.resize(levels, k // 512 * 4)).reshape(k // 512, 4)
    idx = np.arange(k)
    return np.exp2(a[idx // 512, idx % 128 // 32])


BF16 = ml_dtypes.bfloat16


def bf(x):
    return np.asarray(x, np.float32).astype(BF16)


def f64(x):
    return np.asarray(x).astype(np.float64)


E2M1 = np.array([0.0, 0.5, 1.0, 1.5, 2.0, 3.0, 4.0, 6.0, -0.0, -0.5, -1.0, -1.5, -2.0, -3.0, -4.0, -6.0])


def pack_weight(w, fmt):
    k, n = w.shape
    w = f64(bf(w)).reshape(k // 32, 32, n)
    amax = np.abs(w).max(1)
    if fmt == "e4m3":
        byte = np.frexp(amax)[1] - 1 + 127 - 7
    else:
        mant, ex = np.frexp(amax / 6.0)
        byte = np.where(mant > 0.5, ex, ex - 1) + 127
    byte = np.clip(np.where(amax > 0, byte, 1), 1, 254)
    scaled = (w * np.exp2(127.0 - byte)[:, None, :]).reshape(k, n).astype(np.float32)
    by_word = np.ascontiguousarray(scaled.reshape(k // 512, 128, 4, n).transpose(0, 1, 3, 2))
    if fmt == "e4m3":
        words = by_word.astype(ml_dtypes.float8_e4m3fn).view(np.uint8)
    else:
        c = by_word.astype(ml_dtypes.float4_e2m1fn).view(np.uint8) & 0xF
        words = c[..., 0::2] | (c[..., 1::2] << 4)
    return np.ascontiguousarray(words), np.ascontiguousarray(byte.astype(np.uint8).reshape(k // 512, 16, n))


def unpack_weight(words, scales, fmt):
    g, p, n, _ = words.shape
    if fmt == "e4m3":
        vals = np.ascontiguousarray(words).view(ml_dtypes.float8_e4m3fn).astype(np.float64)
    else:
        nib = np.empty((g, p, n, 4), np.uint8)
        nib[..., 0::2] = words & 0xF
        nib[..., 1::2] = words >> 4
        vals = E2M1[nib]
    vals = vals * np.repeat(np.exp2(scales.astype(np.float64) - 127.0), 8, axis=1)[..., None]
    return vals.transpose(0, 1, 3, 2).reshape(g * 512, n)


B, IN, H = 512, 1024, 1024
FMT = "e4m3"


def hard_sigmoid(v):
    return np.clip(v / 6.0 + 0.5, 0.0, 1.0)


def hard_tanh(v):
    return np.clip(v, -1.0, 1.0)


def setup_inputs():
    s, t = mx_kscale(IN), mx_kscale(H)
    input_ = bf(np.random.standard_normal((B, IN)) * s)
    h_0 = bf(np.random.standard_normal((B, H)) * t)
    c_0 = bf(np.random.standard_normal((B, H)))
    W_ih = np.random.standard_normal((4 * H, IN)) * 1.25 / np.sqrt(IN) / s[None, :]
    W_hh = np.random.standard_normal((4 * H, H)) * 1.25 / np.sqrt(H) / t[None, :]
    b_hh = bf(np.random.standard_normal(4 * H) * 0.3)
    W_ih_words, W_ih_scales = pack_weight(np.ascontiguousarray(W_ih.T), FMT)
    W_hh_words, W_hh_scales = pack_weight(np.ascontiguousarray(W_hh.T), FMT)
    return {"input_": input_,
            "h_0": h_0,
            "c_0": c_0,
            "W_ih_words": W_ih_words,
            "W_ih_scales": W_ih_scales,
            "W_hh_words": W_hh_words,
            "W_hh_scales": W_hh_scales,
            "b_hh": b_hh}


def reference(input_, h_0, c_0, W_ih_words, W_ih_scales, W_hh_words, W_hh_scales, b_hh):
    wi = mxq(f64(input_), 1, "e4m3") @ unpack_weight(W_ih_words, W_ih_scales, FMT)
    wh_b = (mxq(f64(h_0), 1, "e4m3") @ unpack_weight(W_hh_words, W_hh_scales, FMT)) + f64(b_hh)
    h_x4 = wh_b + wi
    f, i, o, g = np.split(h_x4, 4, axis=1)
    new = hard_sigmoid(i) * hard_tanh(g)
    old = hard_sigmoid(f) * f64(c_0)
    c_1 = old + new
    h_1 = hard_sigmoid(o) * hard_tanh(c_1)
    return (h_1, c_1)

@@ -1,0 +1,208 @@
+from contextlib import ExitStack
+
+import concourse.mybir as mybir
+from concourse.masks import make_identity
+
+F32 = mybir.dt.float32
+BF16 = mybir.dt.bfloat16
+I32 = mybir.dt.int32
+U32 = mybir.dt.uint32
+U8 = mybir.dt.uint8
+FP8X4 = mybir.dt.float8_e4m3fn_x4
+ALU = mybir.AluOpType
+ACT = mybir.ActivationFunctionType
+
+P = 128
+PACK = 4
+K_PASS = P * PACK
+BATCH = 512
+WIDTH = 1024
+M_TILES = BATCH // P
+GROUPS = WIDTH // K_PASS
+PASSES = 2 * GROUPS
+N_BLOCK = 512
+HALVES = WIDTH // N_BLOCK
+GATE_F, GATE_I, GATE_O, GATE_G = 0, 1, 2, 3
+LAG = 2
+
+FLOPS = 2 * BATCH * (2 * WIDTH) * (4 * WIDTH)
+
+BLOCKS = [(gate, half) for half in range(HALVES) for gate in (GATE_G, GATE_I, GATE_F)] + [
+    (GATE_O, half) for half in range(HALVES)
+]
+
+
+def tile_qlstmcell_kernel(
+    tc, input_, h_0, c_0, W_ih_words, W_ih_scales, W_hh_words, W_hh_scales, b_hh, out_0, out_1
+):
+    nc = tc.nc
+    acts = (input_, h_0)
+    words = (W_ih_words, W_hh_words)
+    scales = (W_ih_scales, W_hh_scales)
+
+    with ExitStack() as stack:
+        keep = stack.enter_context(tc.tile_pool(name="keep", bufs=1))
+        stage = stack.enter_context(tc.tile_pool(name="stage", bufs=4))
+        work = stack.enter_context(tc.tile_pool(name="work", bufs=8))
+        psum = stack.enter_context(tc.psum_pool(name="psum", bufs=8))
+        stack.enter_context(tc.manual_schedule())
+
+        w_planes = keep.tile([P, 4 * WIDTH], U8, align_bytes=64)
+        nc.vector.memset(w_planes[:].bitcast(I32), 0)
+        bias_rows = keep.tile([P, 4 * WIDTH], BF16)
+        nc.vector.memset(bias_rows[:].bitcast(I32), 0)
+        ones = keep.tile([P, P], BF16)
+        nc.vector.memset(ones[:], 1.0)
+        ident = keep.tile([P, P], F32)
+        make_identity(nc, ident[:])
+
+        nc.scalar.dma_start(out=bias_rows[0:1, :], in_=b_hh.rearrange("(o n) -> o n", o=1))
+        raw = keep.tile([P, 2, M_TILES, WIDTH], BF16)
+        for o in range(2):
+            for m in range(M_TILES):
+                nc.sync.dma_start(out=raw[:, o, m, :], in_=acts[o][m * P : (m + 1) * P, :])
+
+        w_words = keep.tile([P, PASSES, 4 * WIDTH], I32, align_bytes=64)
+
+        def load_planes(o):
+            for g in range(GROUPS):
+                k = 4 * (GROUPS * o + g)
+                for q in range(4):
+                    nc.sync.dma_start(
+                        out=w_planes[32 * q + k : 32 * q + k + 4, :].bitcast(I32),
+                        in_=scales[o][g, 4 * q : 4 * q + 4, :].bitcast(I32),
+                    )
+
+        def load_words(o, block):
+            gate, half = block
+            c0 = gate * WIDTH + half * N_BLOCK
+            for g in range(GROUPS):
+                nc.sync.dma_start(
+                    out=w_words[:, GROUPS * o + g, c0 : c0 + N_BLOCK],
+                    in_=words[o][g].rearrange("p n t -> p (n t)")[:, PACK * c0 : PACK * (c0 + N_BLOCK)].bitcast(I32),
+                )
+
+        c0_sb = keep.tile([P, M_TILES, WIDTH], BF16)
+        for o in range(2):
+            load_planes(o)
+            load_words(o, BLOCKS[0])
+        for index in range(1, len(BLOCKS)):
+            for o in range(2):
+                load_words(o, BLOCKS[index])
+            if index == 2:
+                for m in range(M_TILES):
+                    nc.sync.dma_start(out=c0_sb[:, m, :], in_=c_0[m * P : (m + 1) * P, :])
+
+        a_codes = keep.tile([P, 2, M_TILES, GROUPS * P], U32, align_bytes=64)
+        a_planes = keep.tile([P, 2, M_TILES, GROUPS * P], U8, align_bytes=64)
+        for o in range(2):
+            for m in range(M_TILES):
+                pairs = raw[:, o, m, :].bitcast(F32)
+                turned = psum.tile([P, GROUPS * 2, P], F32, tag="bank")
+                for g in range(GROUPS):
+                    for u in range(2):
+                        nc.tensor.transpose(
+                            turned[:, 2 * g + u, :],
+                            pairs[:, 256 * g + u : 256 * (g + 1) : 2],
+                            ident[:],
+                        )
+                grouped = stage.tile([P, GROUPS * P * PACK], BF16, align_bytes=64)
+                nc.scalar.copy(
+                    out=grouped[:].bitcast(F32).rearrange("p (g b u) -> p g b u", g=GROUPS, u=2),
+                    in_=turned[:].rearrange("p (g u) b -> p g b u", u=2),
+                )
+                nc.vector.quantize_mx(
+                    out=a_codes[:, o, m, :].bitcast(FP8X4),
+                    scales=a_planes[:, o, m, :],
+                    in_=grouped[:],
+                )
+
+        bias_all = keep.tile([P, 4 * WIDTH], F32)
+        for index in range(len(BLOCKS)):
+            gate, half = BLOCKS[index]
+            c0 = gate * WIDTH + half * N_BLOCK
+            spread = psum.tile([P, N_BLOCK], F32, tag="bank")
+            nc.tensor.matmul(out=spread[:], lhsT=ones[:], rhs=bias_rows[:, c0 : c0 + N_BLOCK], start=True, stop=True)
+            scale, shift = (1.0, 0.0) if gate == GATE_G else (1.0 / 6.0, 0.5)
+            if index % 2 == 0:
+                nc.vector.tensor_scalar(
+                    out=bias_all[:, c0 : c0 + N_BLOCK], in0=spread[:], scalar1=scale, scalar2=shift,
+                    op0=ALU.mult, op1=ALU.add,
+                )
+            else:
+                nc.scalar.activation(
+                    out=bias_all[:, c0 : c0 + N_BLOCK], in_=spread[:], func=ACT.Copy, bias=shift, scale=scale
+                )
+
+        banks = {}
+        gate_tiles = {}
+
+        def multiply(index):
+            gate, half = BLOCKS[index]
+            c0 = gate * WIDTH + half * N_BLOCK
+            for m in range(M_TILES):
+                banks[(index, m)] = psum.tile([P, N_BLOCK], F32, tag="bank", name="acc")
+            if index == 0:
+                order = [(kk, m) for kk in range(PASSES) for m in range(M_TILES)]
+            else:
+                order = [(kk, m) for m in range(M_TILES) for kk in range(PASSES)]
+            for kk, m in order:
+                o, g = kk // GROUPS, kk % GROUPS
+                nc.tensor.matmul_mx(
+                    out=banks[(index, m)][:],
+                    lhsT=a_codes[:, o, m, g * P : (g + 1) * P].bitcast(FP8X4),
+                    lhsT_scale=a_planes[:, o, m, g * P : (g + 1) * P],
+                    rhs=w_words[:, kk, c0 : c0 + N_BLOCK].bitcast(FP8X4),
+                    rhs_scale=w_planes[4 * kk : P, c0 : c0 + N_BLOCK],
+                    start=(kk == 0),
+                    stop=(kk == PASSES - 1),
+                )
+
+        def leave_psum(index, m):
+            gate, half = BLOCKS[index]
+            c0 = gate * WIDTH + half * N_BLOCK
+            y = work.tile([P, N_BLOCK], F32, tag="gate%d" % gate, name="y")
+            gate_tiles[(gate, half, m)] = y
+            nc.vector.scalar_tensor_tensor(
+                out=y[:], in0=banks[(index, m)][:], scalar=(1.0 if gate == GATE_G else 1.0 / 6.0),
+                in1=bias_all[:, c0 : c0 + N_BLOCK], op0=ALU.mult, op1=ALU.add,
+            )
+            if gate != GATE_G:
+                nc.scalar.activation(out=y[:], in_=y[:], func=ACT.Relu)
+
+        def combine(index, m):
+            gate, half = BLOCKS[index]
+            rows = slice(m * P, (m + 1) * P)
+            cols = slice(half * N_BLOCK, (half + 1) * N_BLOCK)
+            y = gate_tiles[(gate, half, m)]
+            if gate == GATE_G:
+                nc.gpsimd.tensor_scalar(out=y[:], in0=y[:], scalar1=1.0, scalar2=-1.0, op0=ALU.min, op1=ALU.max)
+            elif gate == GATE_I:
+                nc.vector.scalar_tensor_tensor(
+                    out=y[:], in0=y[:], scalar=1.0, in1=gate_tiles[(GATE_G, half, m)][:], op0=ALU.min, op1=ALU.mult
+                )
+            elif gate == GATE_F:
+                nc.vector.scalar_tensor_tensor(
+                    out=y[:], in0=y[:], scalar=1.0, in1=c0_sb[:, m, cols], op0=ALU.min, op1=ALU.mult
+                )
+                nc.gpsimd.tensor_tensor(out=y[:], in0=y[:], in1=gate_tiles[(GATE_I, half, m)][:], op=ALU.add)
+                nc.sync.dma_start(out=out_1[rows, cols], in_=y[:])
+                tanh_c = work.tile([P, N_BLOCK], F32, tag="tanh_c", name="tanh_c")
+                gate_tiles[("tanh_c", half, m)] = tanh_c
+                nc.gpsimd.tensor_scalar(out=tanh_c[:], in0=y[:], scalar1=1.0, scalar2=-1.0, op0=ALU.min, op1=ALU.max)
+            else:
+                nc.vector.scalar_tensor_tensor(
+                    out=y[:], in0=y[:], scalar=1.0, in1=gate_tiles[("tanh_c", half, m)][:], op0=ALU.min, op1=ALU.mult
+                )
+                nc.sync.dma_start(out=out_0[rows, cols], in_=y[:])
+
+        items = [(index, m) for index in range(len(BLOCKS)) for m in range(M_TILES)]
+        for t in range(len(items) + LAG):
+            if t < len(items):
+                index, m = items[t]
+                if m == 0:
+                    multiply(index)
+                leave_psum(index, m)
+            if t >= LAG:
+                index, m = items[t - LAG]
+                combine(index, m)

@@ -23,7 +23,7 @@ PASSES = 2 * GROUPS
 N_BLOCK = 512
 HALVES = WIDTH // N_BLOCK
 GATE_F, GATE_I, GATE_O, GATE_G = 0, 1, 2, 3
-LAG = 2
+LAG = 3
 
 FLOPS = 2 * BATCH * (2 * WIDTH) * (4 * WIDTH)
 
@@ -167,42 +167,64 @@ def tile_qlstmcell_kernel(
                 out=y[:], in0=banks[(index, m)][:], scalar=(1.0 if gate == GATE_G else 1.0 / 6.0),
                 in1=bias_all[:, c0 : c0 + N_BLOCK], op0=ALU.mult, op1=ALU.add,
             )
-            if gate != GATE_G:
+            if gate == GATE_G:
+                nc.scalar.activation(out=y[:], in_=y[:], func=ACT.Relu, bias=1.0, scale=-1.0)
+                nc.scalar.activation(out=y[:], in_=y[:], func=ACT.Relu, bias=2.0, scale=-1.0)
+            elif gate == GATE_I:
+                nc.scalar.activation(out=y[:], in_=y[:], func=ACT.Relu, bias=1.0, scale=-1.0)
+                nc.scalar.activation(out=y[:], in_=y[:], func=ACT.Relu, bias=1.0, scale=-1.0)
+            else:
                 nc.scalar.activation(out=y[:], in_=y[:], func=ACT.Relu)
 
-        def combine(index, m):
+        def product(index, m):
             gate, half = BLOCKS[index]
             rows = slice(m * P, (m + 1) * P)
             cols = slice(half * N_BLOCK, (half + 1) * N_BLOCK)
             y = gate_tiles[(gate, half, m)]
-            if gate == GATE_G:
-                nc.gpsimd.tensor_scalar(out=y[:], in0=y[:], scalar1=1.0, scalar2=-1.0, op0=ALU.min, op1=ALU.max)
-            elif gate == GATE_I:
+            if gate == GATE_I:
                 nc.vector.scalar_tensor_tensor(
-                    out=y[:], in0=y[:], scalar=1.0, in1=gate_tiles[(GATE_G, half, m)][:], op0=ALU.min, op1=ALU.mult
+                    out=y[:], in0=gate_tiles[(GATE_G, half, m)][:], scalar=-1.0, in1=y[:], op0=ALU.add, op1=ALU.mult
                 )
             elif gate == GATE_F:
                 nc.vector.scalar_tensor_tensor(
                     out=y[:], in0=y[:], scalar=1.0, in1=c0_sb[:, m, cols], op0=ALU.min, op1=ALU.mult
                 )
-                nc.gpsimd.tensor_tensor(out=y[:], in0=y[:], in1=gate_tiles[(GATE_I, half, m)][:], op=ALU.add)
-                nc.sync.dma_start(out=out_1[rows, cols], in_=y[:])
-                tanh_c = work.tile([P, N_BLOCK], F32, tag="tanh_c", name="tanh_c")
-                gate_tiles[("tanh_c", half, m)] = tanh_c
-                nc.gpsimd.tensor_scalar(out=tanh_c[:], in0=y[:], scalar1=1.0, scalar2=-1.0, op0=ALU.min, op1=ALU.max)
-            else:
+            elif gate == GATE_O:
                 nc.vector.scalar_tensor_tensor(
                     out=y[:], in0=y[:], scalar=1.0, in1=gate_tiles[("tanh_c", half, m)][:], op0=ALU.min, op1=ALU.mult
                 )
                 nc.sync.dma_start(out=out_0[rows, cols], in_=y[:])
 
+        def new_cell(index, m):
+            gate, half = BLOCKS[index]
+            if gate != GATE_F:
+                return
+            rows = slice(m * P, (m + 1) * P)
+            cols = slice(half * N_BLOCK, (half + 1) * N_BLOCK)
+            y = gate_tiles[(gate, half, m)]
+            nc.vector.tensor_tensor(out=y[:], in0=y[:], in1=gate_tiles[(GATE_I, half, m)][:], op=ALU.add)
+            nc.sync.dma_start(out=out_1[rows, cols], in_=y[:])
+
+        def clip_cell(index, m):
+            gate, half = BLOCKS[index]
+            if gate != GATE_F:
+                return
+            tanh_c = work.tile([P, N_BLOCK], F32, tag="tanh_c", name="tanh_c")
+            gate_tiles[("tanh_c", half, m)] = tanh_c
+            nc.vector.tensor_scalar(
+                out=tanh_c[:], in0=gate_tiles[(gate, half, m)][:], scalar1=1.0, scalar2=-1.0, op0=ALU.min, op1=ALU.max
+            )
+
         items = [(index, m) for index in range(len(BLOCKS)) for m in range(M_TILES)]
-        for t in range(len(items) + LAG):
+        for t in range(len(items) + LAG + 2):
             if t < len(items):
                 index, m = items[t]
                 if m == 0:
                     multiply(index)
                 leave_psum(index, m)
-            if t >= LAG:
-                index, m = items[t - LAG]
-                combine(index, m)
+            if 0 <= t - LAG < len(items):
+                product(*items[t - LAG])
+            if 0 <= t - LAG - 1 < len(items):
+                new_cell(*items[t - LAG - 1])
+            if 0 <= t - LAG - 2 < len(items):
+                clip_cell(*items[t - LAG - 2])

@@ -64,14 +64,16 @@ def tile_qlstmcell_kernel(
 
         w_words = keep.tile([P, PASSES, 4 * WIDTH], I32, align_bytes=64)
 
-        def load_planes(o):
-            for g in range(GROUPS):
-                k = 4 * (GROUPS * o + g)
-                for q in range(4):
-                    nc.sync.dma_start(
-                        out=w_planes[32 * q + k : 32 * q + k + 4, :].bitcast(I32),
-                        in_=scales[o][g, 4 * q : 4 * q + 4, :].bitcast(I32),
-                    )
+        def load_planes():
+            for c in range(2):
+                cols = slice(c * 2 * WIDTH, (c + 1) * 2 * WIDTH)
+                for o in range(2):
+                    for q in range(4):
+                        first = 32 * q + 4 * GROUPS * o
+                        nc.sync.dma_start(
+                            out=w_planes[first : first + 4 * GROUPS, cols].bitcast(I32),
+                            in_=scales[o][:, 4 * q : 4 * q + 4, cols].bitcast(I32),
+                        )
 
         def load_words(o, block):
             gate, half = block
@@ -83,8 +85,8 @@ def tile_qlstmcell_kernel(
                 )
 
         c0_sb = keep.tile([P, M_TILES, WIDTH], BF16)
+        load_planes()
         for o in range(2):
-            load_planes(o)
             load_words(o, BLOCKS[0])
         for index in range(1, len(BLOCKS)):
             for o in range(2):

@@ -23,7 +23,7 @@ PASSES = 2 * GROUPS
 N_BLOCK = 512
 HALVES = WIDTH // N_BLOCK
 GATE_F, GATE_I, GATE_O, GATE_G = 0, 1, 2, 3
-LAG = 3
+RUN = 3
 
 FLOPS = 2 * BATCH * (2 * WIDTH) * (4 * WIDTH)
 
@@ -139,19 +139,14 @@ def tile_qlstmcell_kernel(
         banks = {}
         gate_tiles = {}
 
-        def multiply(index):
-            gate, half = BLOCKS[index]
+        def multiply(gate, half, m):
             c0 = gate * WIDTH + half * N_BLOCK
-            for m in range(M_TILES):
-                banks[(index, m)] = psum.tile([P, N_BLOCK], F32, tag="bank", name="acc")
-            if index == 0:
-                order = [(kk, m) for kk in range(PASSES) for m in range(M_TILES)]
-            else:
-                order = [(kk, m) for m in range(M_TILES) for kk in range(PASSES)]
-            for kk, m in order:
+            acc = psum.tile([P, N_BLOCK], F32, tag="bank", name="acc")
+            banks[(gate, half, m)] = acc
+            for kk in range(PASSES):
                 o, g = kk // GROUPS, kk % GROUPS
                 nc.tensor.matmul_mx(
-                    out=banks[(index, m)][:],
+                    out=acc[:],
                     lhsT=a_codes[:, o, m, g * P : (g + 1) * P].bitcast(FP8X4),
                     lhsT_scale=a_planes[:, o, m, g * P : (g + 1) * P],
                     rhs=w_words[:, kk, c0 : c0 + N_BLOCK].bitcast(FP8X4),
@@ -160,73 +155,72 @@ def tile_qlstmcell_kernel(
                     stop=(kk == PASSES - 1),
                 )
 
-        def leave_psum(index, m):
-            gate, half = BLOCKS[index]
+        def leave_psum(gate, half, m):
             c0 = gate * WIDTH + half * N_BLOCK
             y = work.tile([P, N_BLOCK], F32, tag="gate%d" % gate, name="y")
             gate_tiles[(gate, half, m)] = y
             nc.vector.scalar_tensor_tensor(
-                out=y[:], in0=banks[(index, m)][:], scalar=(1.0 if gate == GATE_G else 1.0 / 6.0),
+                out=y[:], in0=banks[(gate, half, m)][:], scalar=(1.0 if gate == GATE_G else 1.0 / 6.0),
                 in1=bias_all[:, c0 : c0 + N_BLOCK], op0=ALU.mult, op1=ALU.add,
             )
-            if gate == GATE_G:
-                nc.scalar.activation(out=y[:], in_=y[:], func=ACT.Relu, bias=1.0, scale=-1.0)
-                nc.scalar.activation(out=y[:], in_=y[:], func=ACT.Relu, bias=2.0, scale=-1.0)
-            elif gate == GATE_I:
-                nc.scalar.activation(out=y[:], in_=y[:], func=ACT.Relu, bias=1.0, scale=-1.0)
-                nc.scalar.activation(out=y[:], in_=y[:], func=ACT.Relu, bias=1.0, scale=-1.0)
-            else:
+            if gate != GATE_G:
                 nc.scalar.activation(out=y[:], in_=y[:], func=ACT.Relu)
 
-        def product(index, m):
-            gate, half = BLOCKS[index]
+        def new_cell(half, m):
             rows = slice(m * P, (m + 1) * P)
             cols = slice(half * N_BLOCK, (half + 1) * N_BLOCK)
-            y = gate_tiles[(gate, half, m)]
-            if gate == GATE_I:
-                nc.vector.scalar_tensor_tensor(
-                    out=y[:], in0=gate_tiles[(GATE_G, half, m)][:], scalar=-1.0, in1=y[:], op0=ALU.add, op1=ALU.mult
-                )
-            elif gate == GATE_F:
-                nc.vector.scalar_tensor_tensor(
-                    out=y[:], in0=y[:], scalar=1.0, in1=c0_sb[:, m, cols], op0=ALU.min, op1=ALU.mult
-                )
-            elif gate == GATE_O:
-                nc.vector.scalar_tensor_tensor(
-                    out=y[:], in0=y[:], scalar=1.0, in1=gate_tiles[("tanh_c", half, m)][:], op0=ALU.min, op1=ALU.mult
-                )
-                nc.sync.dma_start(out=out_0[rows, cols], in_=y[:])
-
-        def new_cell(index, m):
-            gate, half = BLOCKS[index]
-            if gate != GATE_F:
-                return
-            rows = slice(m * P, (m + 1) * P)
-            cols = slice(half * N_BLOCK, (half + 1) * N_BLOCK)
-            y = gate_tiles[(gate, half, m)]
-            nc.vector.tensor_tensor(out=y[:], in0=y[:], in1=gate_tiles[(GATE_I, half, m)][:], op=ALU.add)
-            nc.sync.dma_start(out=out_1[rows, cols], in_=y[:])
-
-        def clip_cell(index, m):
-            gate, half = BLOCKS[index]
-            if gate != GATE_F:
-                return
+            new = gate_tiles[(GATE_I, half, m)]
+            old = gate_tiles[(GATE_F, half, m)]
+            tanh_g = gate_tiles[(GATE_G, half, m)]
+            nc.vector.tensor_scalar(out=tanh_g[:], in0=tanh_g[:], scalar1=1.0, scalar2=-1.0, op0=ALU.min, op1=ALU.max)
+            nc.vector.scalar_tensor_tensor(
+                out=old[:], in0=old[:], scalar=1.0, in1=c0_sb[:, m, cols], op0=ALU.min, op1=ALU.mult
+            )
+            nc.vector.scalar_tensor_tensor(
+                out=new[:], in0=new[:], scalar=1.0, in1=tanh_g[:], op0=ALU.min, op1=ALU.mult
+            )
+            nc.gpsimd.tensor_tensor(out=old[:], in0=old[:], in1=new[:], op=ALU.add)
+            nc.sync.dma_start(out=out_1[rows, cols], in_=old[:])
             tanh_c = work.tile([P, N_BLOCK], F32, tag="tanh_c", name="tanh_c")
             gate_tiles[("tanh_c", half, m)] = tanh_c
-            nc.vector.tensor_scalar(
-                out=tanh_c[:], in0=gate_tiles[(gate, half, m)][:], scalar1=1.0, scalar2=-1.0, op0=ALU.min, op1=ALU.max
-            )
+            nc.gpsimd.tensor_scalar(out=tanh_c[:], in0=old[:], scalar1=1.0, scalar2=-1.0, op0=ALU.min, op1=ALU.max)
 
-        items = [(index, m) for index in range(len(BLOCKS)) for m in range(M_TILES)]
-        for t in range(len(items) + LAG + 2):
-            if t < len(items):
-                index, m = items[t]
-                if m == 0:
-                    multiply(index)
-                leave_psum(index, m)
-            if 0 <= t - LAG < len(items):
-                product(*items[t - LAG])
-            if 0 <= t - LAG - 1 < len(items):
-                new_cell(*items[t - LAG - 1])
-            if 0 <= t - LAG - 2 < len(items):
-                clip_cell(*items[t - LAG - 2])
+        def new_hidden(half, m):
+            rows = slice(m * P, (m + 1) * P)
+            cols = slice(half * N_BLOCK, (half + 1) * N_BLOCK)
+            y = gate_tiles[(GATE_O, half, m)]
+            nc.vector.scalar_tensor_tensor(
+                out=y[:], in0=y[:], scalar=1.0, in1=gate_tiles[("tanh_c", half, m)][:], op0=ALU.min, op1=ALU.mult
+            )
+            nc.sync.dma_start(out=out_0[rows, cols], in_=y[:])
+
+        pairs = [(half, first) for half in range(HALVES) for first in range(0, M_TILES, 2)]
+        cells = [(half, first + j) for half, first in pairs for j in range(2)]
+        first_banks = [
+            (gate, half, first + j) for half, first in pairs for gate in (GATE_G, GATE_I, GATE_F) for j in range(2)
+        ]
+        last_banks = [(GATE_O, half, m) for half in range(HALVES) for m in range(M_TILES)]
+        turns = len(first_banks) // RUN
+        for turn in range(turns):
+            run = first_banks[turn * RUN : (turn + 1) * RUN]
+            for bank in run:
+                multiply(*bank)
+            if turn >= 2:
+                new_cell(*cells[turn - 2])
+            for bank in run:
+                leave_psum(*bank)
+        left = cells[turns - 2 :]
+        waiting = []
+        for turn in range(len(last_banks) // 2):
+            run = last_banks[2 * turn : 2 * turn + 2]
+            for bank in run:
+                multiply(*bank)
+            if turn < len(left):
+                new_cell(*left[turn])
+            for bank in run:
+                leave_psum(*bank)
+            for half, m in waiting:
+                new_hidden(half, m)
+            waiting = [(half, m) for gate, half, m in run]
+        for half, m in waiting:
+            new_hidden(half, m)

@@ -24,6 +24,7 @@ N_BLOCK = 512
 HALVES = WIDTH // N_BLOCK
 GATE_F, GATE_I, GATE_O, GATE_G = 0, 1, 2, 3
 RUN = 3
+EARLY = 6
 
 FLOPS = 2 * BATCH * (2 * WIDTH) * (4 * WIDTH)
 
@@ -86,9 +87,7 @@ def tile_qlstmcell_kernel(
 
         c0_sb = keep.tile([P, M_TILES, WIDTH], BF16)
         load_planes()
-        for o in range(2):
-            load_words(o, BLOCKS[0])
-        for index in range(1, len(BLOCKS)):
+        for index in range(len(BLOCKS)):
             for o in range(2):
                 load_words(o, BLOCKS[index])
             if index == 2:
@@ -97,33 +96,40 @@ def tile_qlstmcell_kernel(
 
         a_codes = keep.tile([P, 2, M_TILES, GROUPS * P], U32, align_bytes=64)
         a_planes = keep.tile([P, 2, M_TILES, GROUPS * P], U8, align_bytes=64)
-        for o in range(2):
-            for m in range(M_TILES):
-                pairs = raw[:, o, m, :].bitcast(F32)
-                turned = psum.tile([P, GROUPS * 2, P], F32, tag="bank")
-                for g in range(GROUPS):
-                    for u in range(2):
-                        nc.tensor.transpose(
-                            turned[:, 2 * g + u, :],
-                            pairs[:, 256 * g + u : 256 * (g + 1) : 2],
-                            ident[:],
-                        )
-                grouped = stage.tile([P, GROUPS * P * PACK], BF16, align_bytes=64)
-                nc.scalar.copy(
-                    out=grouped[:].bitcast(F32).rearrange("p (g b u) -> p g b u", g=GROUPS, u=2),
-                    in_=turned[:].rearrange("p (g u) b -> p g b u", u=2),
-                )
-                nc.vector.quantize_mx(
-                    out=a_codes[:, o, m, :].bitcast(FP8X4),
-                    scales=a_planes[:, o, m, :],
-                    in_=grouped[:],
-                )
-
         bias_all = keep.tile([P, 4 * WIDTH], F32)
-        for index in range(len(BLOCKS)):
+        regrouped = {}
+
+        def turn_tile(index):
+            o, m = index // M_TILES, index % M_TILES
+            pairs = raw[:, o, m, :].bitcast(F32)
+            turned = psum.tile([P, GROUPS * 2, P], F32, tag="bank", name="turned")
+            for g in range(GROUPS):
+                for u in range(2):
+                    nc.tensor.transpose(
+                        turned[:, 2 * g + u, :],
+                        pairs[:, 256 * g + u : 256 * (g + 1) : 2],
+                        ident[:],
+                    )
+            grouped = stage.tile([P, GROUPS * P * PACK], BF16, align_bytes=64, name="grouped")
+            regrouped[index] = grouped
+            copy = nc.scalar.copy if index % 2 == 0 else nc.vector.tensor_copy
+            copy(
+                out=grouped[:].bitcast(F32).rearrange("p (g b u) -> p g b u", g=GROUPS, u=2),
+                in_=turned[:].rearrange("p (g u) b -> p g b u", u=2),
+            )
+
+        def quantise_tile(index):
+            o, m = index // M_TILES, index % M_TILES
+            nc.vector.quantize_mx(
+                out=a_codes[:, o, m, :].bitcast(FP8X4),
+                scales=a_planes[:, o, m, :],
+                in_=regrouped[index][:],
+            )
+
+        def spread_bias(index):
             gate, half = BLOCKS[index]
             c0 = gate * WIDTH + half * N_BLOCK
-            spread = psum.tile([P, N_BLOCK], F32, tag="bank")
+            spread = psum.tile([P, N_BLOCK], F32, tag="bank", name="spread")
             nc.tensor.matmul(out=spread[:], lhsT=ones[:], rhs=bias_rows[:, c0 : c0 + N_BLOCK], start=True, stop=True)
             scale, shift = (1.0, 0.0) if gate == GATE_G else (1.0 / 6.0, 0.5)
             if index % 2 == 0:
@@ -136,17 +142,30 @@ def tile_qlstmcell_kernel(
                     out=bias_all[:, c0 : c0 + N_BLOCK], in_=spread[:], func=ACT.Copy, bias=shift, scale=scale
                 )
 
+        for index in range(2 * M_TILES):
+            turn_tile(index)
+            spread_bias(index)
+            if index >= 1:
+                quantise_tile(index - 1)
+        quantise_tile(2 * M_TILES - 1)
+
         banks = {}
         gate_tiles = {}
 
-        def multiply(gate, half, m):
-            c0 = gate * WIDTH + half * N_BLOCK
-            acc = psum.tile([P, N_BLOCK], F32, tag="bank", name="acc")
-            banks[(gate, half, m)] = acc
+        def multiply(group):
+            for bank in group:
+                banks[bank] = psum.tile([P, N_BLOCK], F32, tag="bank", name="acc")
             for kk in range(PASSES):
+                for bank in group:
+                    one_pass(bank, kk)
+
+        def one_pass(bank, kk):
+            if True:
+                gate, half, m = bank
+                c0 = gate * WIDTH + half * N_BLOCK
                 o, g = kk // GROUPS, kk % GROUPS
                 nc.tensor.matmul_mx(
-                    out=acc[:],
+                    out=banks[bank][:],
                     lhsT=a_codes[:, o, m, g * P : (g + 1) * P].bitcast(FP8X4),
                     lhsT_scale=a_planes[:, o, m, g * P : (g + 1) * P],
                     rhs=w_words[:, kk, c0 : c0 + N_BLOCK].bitcast(FP8X4),
@@ -201,10 +220,13 @@ def tile_qlstmcell_kernel(
         ]
         last_banks = [(GATE_O, half, m) for half in range(HALVES) for m in range(M_TILES)]
         turns = len(first_banks) // RUN
+        for j in range(0, EARLY, 2):
+            multiply(first_banks[j : j + 2])
         for turn in range(turns):
             run = first_banks[turn * RUN : (turn + 1) * RUN]
             for bank in run:
-                multiply(*bank)
+                if bank not in banks:
+                    multiply([bank])
             if turn >= 2:
                 new_cell(*cells[turn - 2])
             for bank in run:
@@ -214,7 +236,7 @@ def tile_qlstmcell_kernel(
         for turn in range(len(last_banks) // 2):
             run = last_banks[2 * turn : 2 * turn + 2]
             for bank in run:
-                multiply(*bank)
+                multiply([bank])
             if turn < len(left):
                 new_cell(*left[turn])
             for bank in run:

@@ -48,14 +48,21 @@ def tile_qlstmcell_kernel(
         psum = stack.enter_context(tc.psum_pool(name="psum", bufs=8))
         stack.enter_context(tc.manual_schedule())
 
-        w_planes = keep.tile([P, 4 * WIDTH], U8, align_bytes=64)
-        nc.vector.memset(w_planes[:].bitcast(I32), 0)
+        w_planes = keep.tile([P, 2, 4 * WIDTH], U8, align_bytes=64)
+        nc.vector.memset(w_planes[:].rearrange("p o n -> p (o n)").bitcast(I32), 0)
         bias_rows = keep.tile([P, 4 * WIDTH], BF16)
         nc.vector.memset(bias_rows[:].bitcast(I32), 0)
         ones = keep.tile([P, P], BF16)
         nc.vector.memset(ones[:], 1.0)
         ident = keep.tile([P, P], F32)
         make_identity(nc, ident[:])
+
+        for q in range(4):
+            first = 32 * q + 4 * GROUPS
+            nc.gpsimd.dma_start(
+                out=w_planes[first : first + 4 * GROUPS, 1, :].bitcast(F32),
+                in_=scales[1][:, 4 * q : 4 * q + 4, :].bitcast(F32),
+            )
 
         nc.scalar.dma_start(out=bias_rows[0:1, :], in_=b_hh.rearrange("(o n) -> o n", o=1))
         raw = keep.tile([P, 2, M_TILES, WIDTH], BF16)
@@ -68,13 +75,11 @@ def tile_qlstmcell_kernel(
         def load_planes():
             for c in range(2):
                 cols = slice(c * 2 * WIDTH, (c + 1) * 2 * WIDTH)
-                for o in range(2):
-                    for q in range(4):
-                        first = 32 * q + 4 * GROUPS * o
-                        nc.sync.dma_start(
-                            out=w_planes[first : first + 4 * GROUPS, cols].bitcast(I32),
-                            in_=scales[o][:, 4 * q : 4 * q + 4, cols].bitcast(I32),
-                        )
+                for q in range(4):
+                    nc.sync.dma_start(
+                        out=w_planes[32 * q : 32 * q + 4 * GROUPS, 0, cols].bitcast(I32),
+                        in_=scales[0][:, 4 * q : 4 * q + 4, cols].bitcast(I32),
+                    )
 
         def load_words(o, block):
             gate, half = block
@@ -169,7 +174,7 @@ def tile_qlstmcell_kernel(
                     lhsT=a_codes[:, o, m, g * P : (g + 1) * P].bitcast(FP8X4),
                     lhsT_scale=a_planes[:, o, m, g * P : (g + 1) * P],
                     rhs=w_words[:, kk, c0 : c0 + N_BLOCK].bitcast(FP8X4),
-                    rhs_scale=w_planes[4 * kk : P, c0 : c0 + N_BLOCK],
+                    rhs_scale=w_planes[4 * kk : P, o, c0 : c0 + N_BLOCK],
                     start=(kk == 0),
                     stop=(kk == PASSES - 1),
                 )

@@ -23,12 +23,14 @@ PASSES = 2 * GROUPS
 N_BLOCK = 512
 HALVES = WIDTH // N_BLOCK
 GATE_F, GATE_I, GATE_O, GATE_G = 0, 1, 2, 3
+GATE_ORDER = ((GATE_G, GATE_I, GATE_F), (GATE_F, GATE_G, GATE_I))
+BIAS_ORDER = (GATE_G, GATE_I, GATE_F, GATE_O)
 RUN = 3
 EARLY = 6
 
 FLOPS = 2 * BATCH * (2 * WIDTH) * (4 * WIDTH)
 
-BLOCKS = [(gate, half) for half in range(HALVES) for gate in (GATE_G, GATE_I, GATE_F)] + [
+BLOCKS = [(gate, half) for half in range(HALVES) for gate in GATE_ORDER[half]] + [
     (GATE_O, half) for half in range(HALVES)
 ]
 
@@ -48,12 +50,15 @@ def tile_qlstmcell_kernel(
         psum = stack.enter_context(tc.psum_pool(name="psum", bufs=8))
         stack.enter_context(tc.manual_schedule())
 
-        w_planes = keep.tile([P, 2, 4 * WIDTH], U8, align_bytes=64)
-        nc.vector.memset(w_planes[:].rearrange("p o n -> p (o n)").bitcast(I32), 0)
-        bias_rows = keep.tile([P, 4 * WIDTH], BF16)
-        nc.vector.memset(bias_rows[:].bitcast(I32), 0)
         ones = keep.tile([P, P], BF16)
         nc.vector.memset(ones[:], 1.0)
+        w_planes = keep.tile([P, 2, 4 * WIDTH], U8, align_bytes=64)
+        bias_rows = keep.tile([P, 4 * WIDTH], BF16)
+        nc.vector.memset(w_planes[:, 1, :].bitcast(I32), 0)
+        nc.vector.memset(bias_rows[:].bitcast(I32), 0)
+        nc.vector.memset(w_planes[:, 0, :].bitcast(I32), 0)
+        warm = keep.tile([P, 1], F32)
+        nc.scalar.activation(out=warm[:], in_=ones[:, 0:1], func=ACT.Relu)
         ident = keep.tile([P, P], F32)
         make_identity(nc, ident[:])
 
@@ -64,22 +69,21 @@ def tile_qlstmcell_kernel(
                 in_=scales[1][:, 4 * q : 4 * q + 4, :].bitcast(F32),
             )
 
-        nc.scalar.dma_start(out=bias_rows[0:1, :], in_=b_hh.rearrange("(o n) -> o n", o=1))
         raw = keep.tile([P, 2, M_TILES, WIDTH], BF16)
-        for o in range(2):
-            for m in range(M_TILES):
-                nc.sync.dma_start(out=raw[:, o, m, :], in_=acts[o][m * P : (m + 1) * P, :])
+
+        def load_acts():
+            for o in range(2):
+                for m in range(M_TILES):
+                    nc.sync.dma_start(out=raw[:, o, m, :], in_=acts[o][m * P : (m + 1) * P, :])
 
         w_words = keep.tile([P, PASSES, 4 * WIDTH], I32, align_bytes=64)
 
         def load_planes():
-            for c in range(2):
-                cols = slice(c * 2 * WIDTH, (c + 1) * 2 * WIDTH)
-                for q in range(4):
-                    nc.sync.dma_start(
-                        out=w_planes[32 * q : 32 * q + 4 * GROUPS, 0, cols].bitcast(I32),
-                        in_=scales[0][:, 4 * q : 4 * q + 4, cols].bitcast(I32),
-                    )
+            for q in range(4):
+                nc.sync.dma_start(
+                    out=w_planes[32 * q : 32 * q + 4 * GROUPS, 0, :].bitcast(I32),
+                    in_=scales[0][:, 4 * q : 4 * q + 4, :].bitcast(I32),
+                )
 
         def load_words(o, block):
             gate, half = block
@@ -91,6 +95,8 @@ def tile_qlstmcell_kernel(
                 )
 
         c0_sb = keep.tile([P, M_TILES, WIDTH], BF16)
+        load_acts()
+        nc.sync.dma_start(out=bias_rows[0:1, :], in_=b_hh.rearrange("(o n) -> o n", o=1))
         load_planes()
         for index in range(len(BLOCKS)):
             for o in range(2):
@@ -101,7 +107,8 @@ def tile_qlstmcell_kernel(
 
         a_codes = keep.tile([P, 2, M_TILES, GROUPS * P], U32, align_bytes=64)
         a_planes = keep.tile([P, 2, M_TILES, GROUPS * P], U8, align_bytes=64)
-        bias_all = keep.tile([P, 4 * WIDTH], F32)
+        bias_all = keep.tile([P, 4 * WIDTH], BF16)
+        spreads = {}
         regrouped = {}
 
         def turn_tile(index):
@@ -132,27 +139,24 @@ def tile_qlstmcell_kernel(
             )
 
         def spread_bias(index):
-            gate, half = BLOCKS[index]
+            gate, half = BIAS_ORDER[index // 2], index % 2
             c0 = gate * WIDTH + half * N_BLOCK
-            spread = psum.tile([P, N_BLOCK], F32, tag="bank", name="spread")
-            nc.tensor.matmul(out=spread[:], lhsT=ones[:], rhs=bias_rows[:, c0 : c0 + N_BLOCK], start=True, stop=True)
-            scale, shift = (1.0, 0.0) if gate == GATE_G else (1.0 / 6.0, 0.5)
-            if index % 2 == 0:
-                nc.vector.tensor_scalar(
-                    out=bias_all[:, c0 : c0 + N_BLOCK], in0=spread[:], scalar1=scale, scalar2=shift,
-                    op0=ALU.mult, op1=ALU.add,
-                )
-            else:
-                nc.scalar.activation(
-                    out=bias_all[:, c0 : c0 + N_BLOCK], in_=spread[:], func=ACT.Copy, bias=shift, scale=scale
-                )
+            if half == 0:
+                spreads[gate] = psum.tile([P, WIDTH], BF16, tag="bank", name="spread")
+            nc.tensor.matmul(
+                out=spreads[gate][:, half * N_BLOCK : (half + 1) * N_BLOCK], lhsT=ones[:],
+                rhs=bias_rows[:, c0 : c0 + N_BLOCK], start=True, stop=True,
+            )
+            if half == 1:
+                nc.scalar.copy(out=bias_all[:, gate * WIDTH : (gate + 1) * WIDTH], in_=spreads[gate][:])
 
         for index in range(2 * M_TILES):
             turn_tile(index)
-            spread_bias(index)
             if index >= 1:
                 quantise_tile(index - 1)
         quantise_tile(2 * M_TILES - 1)
+        for index in range(2 * M_TILES):
+            spread_bias(index)
 
         banks = {}
         gate_tiles = {}
@@ -184,25 +188,34 @@ def tile_qlstmcell_kernel(
             y = work.tile([P, N_BLOCK], F32, tag="gate%d" % gate, name="y")
             gate_tiles[(gate, half, m)] = y
             nc.vector.scalar_tensor_tensor(
-                out=y[:], in0=banks[(gate, half, m)][:], scalar=(1.0 if gate == GATE_G else 1.0 / 6.0),
+                out=y[:], in0=banks[(gate, half, m)][:], scalar=1.0,
                 in1=bias_all[:, c0 : c0 + N_BLOCK], op0=ALU.mult, op1=ALU.add,
             )
             if gate != GATE_G:
-                nc.scalar.activation(out=y[:], in_=y[:], func=ACT.Relu)
+                nc.scalar.activation(out=y[:], in_=y[:], func=ACT.Relu, bias=0.5, scale=1.0 / 6.0)
 
-        def new_cell(half, m):
+        def clip_g(half, m):
+            tanh_g = gate_tiles[(GATE_G, half, m)]
+            nc.vector.tensor_scalar(out=tanh_g[:], in0=tanh_g[:], scalar1=1.0, scalar2=-1.0, op0=ALU.min, op1=ALU.max)
+
+        def old_part(half, m):
+            old = gate_tiles[(GATE_F, half, m)]
+            cols = slice(half * N_BLOCK, (half + 1) * N_BLOCK)
+            nc.vector.scalar_tensor_tensor(
+                out=old[:], in0=old[:], scalar=1.0, in1=c0_sb[:, m, cols], op0=ALU.min, op1=ALU.mult
+            )
+
+        def new_part(half, m):
+            new = gate_tiles[(GATE_I, half, m)]
+            nc.vector.scalar_tensor_tensor(
+                out=new[:], in0=new[:], scalar=1.0, in1=gate_tiles[(GATE_G, half, m)][:], op0=ALU.min, op1=ALU.mult
+            )
+
+        def sum_cell(half, m):
             rows = slice(m * P, (m + 1) * P)
             cols = slice(half * N_BLOCK, (half + 1) * N_BLOCK)
             new = gate_tiles[(GATE_I, half, m)]
             old = gate_tiles[(GATE_F, half, m)]
-            tanh_g = gate_tiles[(GATE_G, half, m)]
-            nc.vector.tensor_scalar(out=tanh_g[:], in0=tanh_g[:], scalar1=1.0, scalar2=-1.0, op0=ALU.min, op1=ALU.max)
-            nc.vector.scalar_tensor_tensor(
-                out=old[:], in0=old[:], scalar=1.0, in1=c0_sb[:, m, cols], op0=ALU.min, op1=ALU.mult
-            )
-            nc.vector.scalar_tensor_tensor(
-                out=new[:], in0=new[:], scalar=1.0, in1=tanh_g[:], op0=ALU.min, op1=ALU.mult
-            )
             nc.gpsimd.tensor_tensor(out=old[:], in0=old[:], in1=new[:], op=ALU.add)
             nc.sync.dma_start(out=out_1[rows, cols], in_=old[:])
             tanh_c = work.tile([P, N_BLOCK], F32, tag="tanh_c", name="tanh_c")
@@ -221,33 +234,41 @@ def tile_qlstmcell_kernel(
         pairs = [(half, first) for half in range(HALVES) for first in range(0, M_TILES, 2)]
         cells = [(half, first + j) for half, first in pairs for j in range(2)]
         first_banks = [
-            (gate, half, first + j) for half, first in pairs for gate in (GATE_G, GATE_I, GATE_F) for j in range(2)
+            (gate, half, first + j) for half, first in pairs for gate in GATE_ORDER[half] for j in range(2)
         ]
         last_banks = [(GATE_O, half, m) for half in range(HALVES) for m in range(M_TILES)]
-        turns = len(first_banks) // RUN
+        runs = [first_banks[j : j + RUN] for j in range(0, len(first_banks), RUN)]
+        runs += [last_banks[j : j + 2] for j in range(0, len(last_banks), 2)]
+        follow = {GATE_G: clip_g, GATE_I: new_part, GATE_F: old_part}
+        plan = [[] for run in runs]
+        for turn, run in enumerate(runs[: len(first_banks) // RUN]):
+            for place, bank in enumerate(run):
+                late = 1 if (place == RUN - 1 and bank[0] != GATE_G) else 0
+                plan[turn + 1 + late].append(bank)
+        begun = set()
+        ripe = set()
+        waiting = []
         for j in range(0, EARLY, 2):
             multiply(first_banks[j : j + 2])
-        for turn in range(turns):
-            run = first_banks[turn * RUN : (turn + 1) * RUN]
+        for turn, run in enumerate(runs):
             for bank in run:
                 if bank not in banks:
                     multiply([bank])
-            if turn >= 2:
-                new_cell(*cells[turn - 2])
+            closing = []
+            for bank in plan[turn]:
+                if bank[0] != GATE_G and bank[1:] in begun:
+                    closing.append(bank)
+                else:
+                    follow[bank[0]](*bank[1:])
+                    if bank[0] != GATE_G:
+                        begun.add(bank[1:])
+            for bank in closing:
+                follow[bank[0]](*bank[1:])
+                sum_cell(*bank[1:])
             for bank in run:
                 leave_psum(*bank)
-        left = cells[turns - 2 :]
-        waiting = []
-        for turn in range(len(last_banks) // 2):
-            run = last_banks[2 * turn : 2 * turn + 2]
-            for bank in run:
-                multiply([bank])
-            if turn < len(left):
-                new_cell(*left[turn])
-            for bank in run:
-                leave_psum(*bank)
-            for half, m in waiting:
-                new_hidden(half, m)
-            waiting = [(half, m) for gate, half, m in run]
-        for half, m in waiting:
-            new_hidden(half, m)
+            for cell in waiting:
+                new_hidden(*cell)
+            waiting = [bank[1:] for bank in run if bank[0] == GATE_O]
+        for cell in waiting:
+            new_hidden(*cell)

@@ -25,6 +25,8 @@ HALVES = WIDTH // N_BLOCK
 GATE_F, GATE_I, GATE_O, GATE_G = 0, 1, 2, 3
 GATE_ORDER = ((GATE_G, GATE_I, GATE_F), (GATE_F, GATE_G, GATE_I))
 BIAS_ORDER = (GATE_G, GATE_I, GATE_F, GATE_O)
+BIAS_ROWS = 32
+WARM_UP = 14
 RUN = 3
 EARLY = 6
 
@@ -52,15 +54,22 @@ def tile_qlstmcell_kernel(
 
         ones = keep.tile([P, P], BF16)
         nc.vector.memset(ones[:], 1.0)
-        w_planes = keep.tile([P, 2, 4 * WIDTH], U8, align_bytes=64)
-        bias_rows = keep.tile([P, 4 * WIDTH], BF16)
+        bias_rows = keep.tile([P, P], BF16)
+        nc.sync.dma_start(out=bias_rows[0:BIAS_ROWS, :], in_=b_hh.rearrange("(r n) -> r n", r=BIAS_ROWS))
+        nc.vector.memset(bias_rows[32:64, :], 0.0)
+        nc.vector.memset(bias_rows[64:P, :], 0.0)
+        w_planes = keep.tile([P, 2, 4 * WIDTH], U8, align_bytes=256)
         nc.vector.memset(w_planes[:, 1, :].bitcast(I32), 0)
-        nc.vector.memset(bias_rows[:].bitcast(I32), 0)
         nc.vector.memset(w_planes[:, 0, :].bitcast(I32), 0)
         warm = keep.tile([P, 1], F32)
         nc.scalar.activation(out=warm[:], in_=ones[:, 0:1], func=ACT.Relu)
+        unread = psum.tile([P, P], F32, tag="bank", name="unread")
+        for j in range(WARM_UP):
+            nc.tensor.matmul(out=unread[:], lhsT=ones[:], rhs=ones[:], start=True, stop=True)
         ident = keep.tile([P, P], F32)
         make_identity(nc, ident[:])
+        pick = keep.tile([P, P], BF16)
+        make_identity(nc, pick[:])
 
         for q in range(4):
             first = 32 * q + 4 * GROUPS
@@ -76,7 +85,7 @@ def tile_qlstmcell_kernel(
                 for m in range(M_TILES):
                     nc.sync.dma_start(out=raw[:, o, m, :], in_=acts[o][m * P : (m + 1) * P, :])
 
-        w_words = keep.tile([P, PASSES, 4 * WIDTH], I32, align_bytes=64)
+        w_words = keep.tile([P, PASSES, 4 * WIDTH], I32, align_bytes=256)
 
         def load_planes():
             for q in range(4):
@@ -96,7 +105,6 @@ def tile_qlstmcell_kernel(
 
         c0_sb = keep.tile([P, M_TILES, WIDTH], BF16)
         load_acts()
-        nc.sync.dma_start(out=bias_rows[0:1, :], in_=b_hh.rearrange("(o n) -> o n", o=1))
         load_planes()
         for index in range(len(BLOCKS)):
             for o in range(2):
@@ -105,8 +113,8 @@ def tile_qlstmcell_kernel(
                 for m in range(M_TILES):
                     nc.sync.dma_start(out=c0_sb[:, m, :], in_=c_0[m * P : (m + 1) * P, :])
 
-        a_codes = keep.tile([P, 2, M_TILES, GROUPS * P], U32, align_bytes=64)
-        a_planes = keep.tile([P, 2, M_TILES, GROUPS * P], U8, align_bytes=64)
+        a_codes = keep.tile([P, 2, M_TILES, GROUPS * P], U32, align_bytes=256)
+        a_planes = keep.tile([P, 2, M_TILES, GROUPS * P], U8, align_bytes=256)
         bias_all = keep.tile([P, 4 * WIDTH], BF16)
         spreads = {}
         regrouped = {}
@@ -143,20 +151,21 @@ def tile_qlstmcell_kernel(
             c0 = gate * WIDTH + half * N_BLOCK
             if half == 0:
                 spreads[gate] = psum.tile([P, WIDTH], BF16, tag="bank", name="spread")
-            nc.tensor.matmul(
-                out=spreads[gate][:, half * N_BLOCK : (half + 1) * N_BLOCK], lhsT=ones[:],
-                rhs=bias_rows[:, c0 : c0 + N_BLOCK], start=True, stop=True,
-            )
+            for q in range(N_BLOCK // P):
+                row = c0 // P + q
+                nc.tensor.matmul(
+                    out=spreads[gate][:, half * N_BLOCK + q * P : half * N_BLOCK + (q + 1) * P],
+                    lhsT=pick[:, row : row + 1].to_broadcast([P, P]), rhs=bias_rows[:], start=True, stop=True,
+                )
             if half == 1:
                 nc.scalar.copy(out=bias_all[:, gate * WIDTH : (gate + 1) * WIDTH], in_=spreads[gate][:])
 
         for index in range(2 * M_TILES):
             turn_tile(index)
+            spread_bias(index)
             if index >= 1:
                 quantise_tile(index - 1)
         quantise_tile(2 * M_TILES - 1)
-        for index in range(2 * M_TILES):
-            spread_bias(index)
 
         banks = {}
         gate_tiles = {}

@@ -247,7 +247,7 @@ def tile_qlstmcell_kernel(
         ]
         last_banks = [(GATE_O, half, m) for half in range(HALVES) for m in range(M_TILES)]
         runs = [first_banks[j : j + RUN] for j in range(0, len(first_banks), RUN)]
-        runs += [last_banks[j : j + 2] for j in range(0, len(last_banks), 2)]
+        runs += [[bank] for bank in last_banks]
         follow = {GATE_G: clip_g, GATE_I: new_part, GATE_F: old_part}
         plan = [[] for run in runs]
         for turn, run in enumerate(runs[: len(first_banks) // RUN]):

@@ -26,6 +26,7 @@ GATE_F, GATE_I, GATE_O, GATE_G = 0, 1, 2, 3
 GATE_ORDER = ((GATE_G, GATE_I, GATE_F), (GATE_F, GATE_G, GATE_I))
 BIAS_ORDER = (GATE_G, GATE_I, GATE_F, GATE_O)
 BIAS_ROWS = 32
+LAST_WIDTH = 256
 WARM_UP = 14
 RUN = 3
 EARLY = 6
@@ -35,6 +36,9 @@ FLOPS = 2 * BATCH * (2 * WIDTH) * (4 * WIDTH)
 BLOCKS = [(gate, half) for half in range(HALVES) for gate in GATE_ORDER[half]] + [
     (GATE_O, half) for half in range(HALVES)
 ]
+
+
+PLANES_AHEAD = {(GATE_G, 0): (GATE_G, 1), (GATE_I, 0): (GATE_F, 2), (GATE_O, 0): (GATE_O, 1)}
 
 
 def tile_qlstmcell_kernel(
@@ -87,11 +91,12 @@ def tile_qlstmcell_kernel(
 
         w_words = keep.tile([P, PASSES, 4 * WIDTH], I32, align_bytes=256)
 
-        def load_planes():
+        def load_planes(first_gate, gates):
+            cols = slice(first_gate * WIDTH, (first_gate + gates) * WIDTH)
             for q in range(4):
                 nc.sync.dma_start(
-                    out=w_planes[32 * q : 32 * q + 4 * GROUPS, 0, :].bitcast(I32),
-                    in_=scales[0][:, 4 * q : 4 * q + 4, :].bitcast(I32),
+                    out=w_planes[32 * q : 32 * q + 4 * GROUPS, 0, cols].bitcast(I32),
+                    in_=scales[0][:, 4 * q : 4 * q + 4, cols].bitcast(I32),
                 )
 
         def load_words(o, block):
@@ -105,8 +110,9 @@ def tile_qlstmcell_kernel(
 
         c0_sb = keep.tile([P, M_TILES, WIDTH], BF16)
         load_acts()
-        load_planes()
         for index in range(len(BLOCKS)):
+            if BLOCKS[index] in PLANES_AHEAD:
+                load_planes(*PLANES_AHEAD[BLOCKS[index]])
             for o in range(2):
                 load_words(o, BLOCKS[index])
             if index == 2:
@@ -172,33 +178,34 @@ def tile_qlstmcell_kernel(
 
         def multiply(group):
             for bank in group:
-                banks[bank] = psum.tile([P, N_BLOCK], F32, tag="bank", name="acc")
+                banks[bank] = psum.tile([P, bank[4]], F32, tag="bank", name="acc")
             for kk in range(PASSES):
                 for bank in group:
                     one_pass(bank, kk)
 
         def one_pass(bank, kk):
             if True:
-                gate, half, m = bank
-                c0 = gate * WIDTH + half * N_BLOCK
+                gate, half, m, first, width = bank
+                c0 = gate * WIDTH + half * N_BLOCK + first
                 o, g = kk // GROUPS, kk % GROUPS
                 nc.tensor.matmul_mx(
                     out=banks[bank][:],
                     lhsT=a_codes[:, o, m, g * P : (g + 1) * P].bitcast(FP8X4),
                     lhsT_scale=a_planes[:, o, m, g * P : (g + 1) * P],
-                    rhs=w_words[:, kk, c0 : c0 + N_BLOCK].bitcast(FP8X4),
-                    rhs_scale=w_planes[4 * kk : P, o, c0 : c0 + N_BLOCK],
+                    rhs=w_words[:, kk, c0 : c0 + width].bitcast(FP8X4),
+                    rhs_scale=w_planes[4 * kk : P, o, c0 : c0 + width],
                     start=(kk == 0),
                     stop=(kk == PASSES - 1),
                 )
 
-        def leave_psum(gate, half, m):
-            c0 = gate * WIDTH + half * N_BLOCK
-            y = work.tile([P, N_BLOCK], F32, tag="gate%d" % gate, name="y")
-            gate_tiles[(gate, half, m)] = y
+        def leave_psum(bank):
+            gate, half, m, first, width = bank
+            c0 = gate * WIDTH + half * N_BLOCK + first
+            y = work.tile([P, width], F32, tag="gate%d" % gate, name="y")
+            gate_tiles[(gate, half, m) if gate != GATE_O else bank] = y
             nc.vector.scalar_tensor_tensor(
-                out=y[:], in0=banks[(gate, half, m)][:], scalar=1.0,
-                in1=bias_all[:, c0 : c0 + N_BLOCK], op0=ALU.mult, op1=ALU.add,
+                out=y[:], in0=banks[bank][:], scalar=1.0,
+                in1=bias_all[:, c0 : c0 + width], op0=ALU.mult, op1=ALU.add,
             )
             if gate != GATE_G:
                 nc.scalar.activation(out=y[:], in_=y[:], func=ACT.Relu, bias=0.5, scale=1.0 / 6.0)
@@ -231,23 +238,30 @@ def tile_qlstmcell_kernel(
             gate_tiles[("tanh_c", half, m)] = tanh_c
             nc.gpsimd.tensor_scalar(out=tanh_c[:], in0=old[:], scalar1=1.0, scalar2=-1.0, op0=ALU.min, op1=ALU.max)
 
-        def new_hidden(half, m):
+        def new_hidden(bank):
+            gate, half, m, first, width = bank
             rows = slice(m * P, (m + 1) * P)
-            cols = slice(half * N_BLOCK, (half + 1) * N_BLOCK)
-            y = gate_tiles[(GATE_O, half, m)]
+            cols = slice(half * N_BLOCK + first, half * N_BLOCK + first + width)
+            y = gate_tiles[bank]
             nc.vector.scalar_tensor_tensor(
-                out=y[:], in0=y[:], scalar=1.0, in1=gate_tiles[("tanh_c", half, m)][:], op0=ALU.min, op1=ALU.mult
+                out=y[:], in0=y[:], scalar=1.0, in1=gate_tiles[("tanh_c", half, m)][:, first : first + width],
+                op0=ALU.min, op1=ALU.mult,
             )
             nc.sync.dma_start(out=out_0[rows, cols], in_=y[:])
 
         pairs = [(half, first) for half in range(HALVES) for first in range(0, M_TILES, 2)]
         cells = [(half, first + j) for half, first in pairs for j in range(2)]
-        first_banks = [
-            (gate, half, first + j) for half, first in pairs for gate in GATE_ORDER[half] for j in range(2)
+        first_banks = [(GATE_ORDER[0][0], 0, m, 0, N_BLOCK) for m in range(M_TILES)]
+        first_banks += [
+            (gate, half, first + j, 0, N_BLOCK)
+            for half, first in pairs for gate in GATE_ORDER[half][1 - half :] for j in range(2)
         ]
-        last_banks = [(GATE_O, half, m) for half in range(HALVES) for m in range(M_TILES)]
+        last_banks = [(GATE_O, half, m, 0, N_BLOCK) for half in range(HALVES) for m in range(M_TILES)]
+        gate, half, m = last_banks.pop()[0:3]
+        last_banks += [(gate, half, m, first, LAST_WIDTH) for first in range(0, N_BLOCK, LAST_WIDTH)]
         runs = [first_banks[j : j + RUN] for j in range(0, len(first_banks), RUN)]
-        runs += [[bank] for bank in last_banks]
+        runs += [[bank] for bank in last_banks if bank[4] == N_BLOCK]
+        runs.append([bank for bank in last_banks if bank[4] != N_BLOCK])
         follow = {GATE_G: clip_g, GATE_I: new_part, GATE_F: old_part}
         plan = [[] for run in runs]
         for turn, run in enumerate(runs[: len(first_banks) // RUN]):
@@ -257,27 +271,28 @@ def tile_qlstmcell_kernel(
         begun = set()
         ripe = set()
         waiting = []
-        for j in range(0, EARLY, 2):
-            multiply(first_banks[j : j + 2])
+        multiply(first_banks[0:M_TILES])
+        held = []
         for turn, run in enumerate(runs):
             for bank in run:
                 if bank not in banks:
                     multiply([bank])
-            closing = []
+            closing = held
             for bank in plan[turn]:
-                if bank[0] != GATE_G and bank[1:] in begun:
+                if bank[0] != GATE_G and bank[1:3] in begun:
                     closing.append(bank)
                 else:
-                    follow[bank[0]](*bank[1:])
+                    follow[bank[0]](*bank[1:3])
                     if bank[0] != GATE_G:
-                        begun.add(bank[1:])
-            for bank in closing:
-                follow[bank[0]](*bank[1:])
-                sum_cell(*bank[1:])
+                        begun.add(bank[1:3])
+            held = closing[1:]
+            for bank in closing[:1]:
+                follow[bank[0]](*bank[1:3])
+                sum_cell(*bank[1:3])
             for bank in run:
-                leave_psum(*bank)
-            for cell in waiting:
-                new_hidden(*cell)
-            waiting = [bank[1:] for bank in run if bank[0] == GATE_O]
-        for cell in waiting:
-            new_hidden(*cell)
+                leave_psum(bank)
+            for bank in waiting:
+                new_hidden(bank)
+            waiting = [bank for bank in run if bank[0] == GATE_O]
+        for bank in waiting:
+            new_hidden(bank)

@@ -167,8 +167,10 @@ def tile_qlstmcell_kernel(
                 nc.scalar.copy(out=bias_all[:, gate * WIDTH : (gate + 1) * WIDTH], in_=spreads[gate][:])
 
         for index in range(2 * M_TILES):
+            if index % 2 == 0:
+                spread_bias(index)
+                spread_bias(index + 1)
             turn_tile(index)
-            spread_bias(index)
             if index >= 1:
                 quantise_tile(index - 1)
         quantise_tile(2 * M_TILES - 1)

@@ -53,6 +53,7 @@ def tile_qlstmcell_kernel(
         keep = stack.enter_context(tc.tile_pool(name="keep", bufs=1))
         stage = stack.enter_context(tc.tile_pool(name="stage", bufs=4))
         work = stack.enter_context(tc.tile_pool(name="work", bufs=8))
+        far = stack.enter_context(tc.tile_pool(name="far", bufs=1))
         psum = stack.enter_context(tc.psum_pool(name="psum", bufs=8))
         stack.enter_context(tc.manual_schedule())
 
@@ -119,8 +120,8 @@ def tile_qlstmcell_kernel(
                 for m in range(M_TILES):
                     nc.sync.dma_start(out=c0_sb[:, m, :], in_=c_0[m * P : (m + 1) * P, :])
 
-        a_codes = keep.tile([P, 2, M_TILES, GROUPS * P], U32, align_bytes=256)
-        a_planes = keep.tile([P, 2, M_TILES, GROUPS * P], U8, align_bytes=256)
+        a_codes = far.tile([P, 2, M_TILES, GROUPS * P], U32, align_bytes=256)
+        a_planes = far.tile([P, 2, M_TILES, GROUPS * P], U8, align_bytes=256)
         bias_all = keep.tile([P, 4 * WIDTH], BF16)
         spreads = {}
         regrouped = {}

@@ -276,6 +276,7 @@ def tile_qlstmcell_kernel(
         waiting = []
         multiply(first_banks[0:M_TILES])
         held = []
+        summed = []
         for turn, run in enumerate(runs):
             for bank in run:
                 if bank not in banks:
@@ -288,10 +289,12 @@ def tile_qlstmcell_kernel(
                     follow[bank[0]](*bank[1:3])
                     if bank[0] != GATE_G:
                         begun.add(bank[1:3])
-            held = closing[1:]
-            for bank in closing[:1]:
+            room = 1 if summed else 2
+            held = closing[room:]
+            for bank in closing[:room]:
                 follow[bank[0]](*bank[1:3])
                 sum_cell(*bank[1:3])
+                summed.append(bank[1:3])
             for bank in run:
                 leave_psum(bank)
             for bank in waiting:

from contextlib import ExitStack

import concourse.mybir as mybir
from concourse.masks import make_identity

F32 = mybir.dt.float32
BF16 = mybir.dt.bfloat16
I32 = mybir.dt.int32
U32 = mybir.dt.uint32
U8 = mybir.dt.uint8
FP8X4 = mybir.dt.float8_e4m3fn_x4
ALU = mybir.AluOpType
ACT = mybir.ActivationFunctionType

P = 128
PACK = 4
K_PASS = P * PACK
BATCH = 512
WIDTH = 1024
M_TILES = BATCH // P
GROUPS = WIDTH // K_PASS
PASSES = 2 * GROUPS
N_BLOCK = 512
HALVES = WIDTH // N_BLOCK
GATE_F, GATE_I, GATE_O, GATE_G = 0, 1, 2, 3
GATE_ORDER = ((GATE_G, GATE_I, GATE_F), (GATE_F, GATE_G, GATE_I))
BIAS_ORDER = (GATE_G, GATE_I, GATE_F, GATE_O)
BIAS_ROWS = 32
LAST_WIDTH = 256
WARM_UP = 14
RUN = 3
EARLY = 6

FLOPS = 2 * BATCH * (2 * WIDTH) * (4 * WIDTH)

BLOCKS = [(gate, half) for half in range(HALVES) for gate in GATE_ORDER[half]] + [
    (GATE_O, half) for half in range(HALVES)
]


PLANES_AHEAD = {(GATE_G, 0): (GATE_G, 1), (GATE_I, 0): (GATE_F, 2), (GATE_O, 0): (GATE_O, 1)}


def tile_qlstmcell_kernel(
    tc, input_, h_0, c_0, W_ih_words, W_ih_scales, W_hh_words, W_hh_scales, b_hh, out_0, out_1
):
    nc = tc.nc
    acts = (input_, h_0)
    words = (W_ih_words, W_hh_words)
    scales = (W_ih_scales, W_hh_scales)

    with ExitStack() as stack:
        keep = stack.enter_context(tc.tile_pool(name="keep", bufs=1))
        stage = stack.enter_context(tc.tile_pool(name="stage", bufs=4))
        work = stack.enter_context(tc.tile_pool(name="work", bufs=8))
        far = stack.enter_context(tc.tile_pool(name="far", bufs=1))
        psum = stack.enter_context(tc.psum_pool(name="psum", bufs=8))
        stack.enter_context(tc.manual_schedule())

        ones = keep.tile([P, P], BF16)
        nc.vector.memset(ones[:], 1.0)
        bias_rows = keep.tile([P, P], BF16)
        nc.sync.dma_start(out=bias_rows[0:BIAS_ROWS, :], in_=b_hh.rearrange("(r n) -> r n", r=BIAS_ROWS))
        nc.vector.memset(bias_rows[32:64, :], 0.0)
        nc.vector.memset(bias_rows[64:P, :], 0.0)
        w_planes = keep.tile([P, 2, 4 * WIDTH], U8, align_bytes=256)
        nc.vector.memset(w_planes[:, 1, :].bitcast(I32), 0)
        nc.vector.memset(w_planes[:, 0, :].bitcast(I32), 0)
        warm = keep.tile([P, 1], F32)
        nc.scalar.activation(out=warm[:], in_=ones[:, 0:1], func=ACT.Relu)
        unread = psum.tile([P, P], F32, tag="bank", name="unread")
        for j in range(WARM_UP):
            nc.tensor.matmul(out=unread[:], lhsT=ones[:], rhs=ones[:], start=True, stop=True)
        ident = keep.tile([P, P], F32)
        make_identity(nc, ident[:])
        pick = keep.tile([P, P], BF16)
        make_identity(nc, pick[:])

        for q in range(4):
            first = 32 * q + 4 * GROUPS
            nc.gpsimd.dma_start(
                out=w_planes[first : first + 4 * GROUPS, 1, :].bitcast(F32),
                in_=scales[1][:, 4 * q : 4 * q + 4, :].bitcast(F32),
            )

        raw = keep.tile([P, 2, M_TILES, WIDTH], BF16)

        def load_acts():
            for o in range(2):
                for m in range(M_TILES):
                    nc.sync.dma_start(out=raw[:, o, m, :], in_=acts[o][m * P : (m + 1) * P, :])

        w_words = keep.tile([P, PASSES, 4 * WIDTH], I32, align_bytes=256)

        def load_planes(first_gate, gates):
            cols = slice(first_gate * WIDTH, (first_gate + gates) * WIDTH)
            for q in range(4):
                nc.sync.dma_start(
                    out=w_planes[32 * q : 32 * q + 4 * GROUPS, 0, cols].bitcast(I32),
                    in_=scales[0][:, 4 * q : 4 * q + 4, cols].bitcast(I32),
                )

        def load_words(o, block):
            gate, half = block
            c0 = gate * WIDTH + half * N_BLOCK
            for g in range(GROUPS):
                nc.sync.dma_start(
                    out=w_words[:, GROUPS * o + g, c0 : c0 + N_BLOCK],
                    in_=words[o][g].rearrange("p n t -> p (n t)")[:, PACK * c0 : PACK * (c0 + N_BLOCK)].bitcast(I32),
                )

        c0_sb = keep.tile([P, M_TILES, WIDTH], BF16)
        load_acts()
        for index in range(len(BLOCKS)):
            if BLOCKS[index] in PLANES_AHEAD:
                load_planes(*PLANES_AHEAD[BLOCKS[index]])
            for o in range(2):
                load_words(o, BLOCKS[index])
            if index == 2:
                for m in range(M_TILES):
                    nc.sync.dma_start(out=c0_sb[:, m, :], in_=c_0[m * P : (m + 1) * P, :])

        a_codes = far.tile([P, 2, M_TILES, GROUPS * P], U32, align_bytes=256)
        a_planes = far.tile([P, 2, M_TILES, GROUPS * P], U8, align_bytes=256)
        bias_all = keep.tile([P, 4 * WIDTH], BF16)
        spreads = {}
        regrouped = {}

        def turn_tile(index):
            o, m = index // M_TILES, index % M_TILES
            pairs = raw[:, o, m, :].bitcast(F32)
            turned = psum.tile([P, GROUPS * 2, P], F32, tag="bank", name="turned")
            for g in range(GROUPS):
                for u in range(2):
                    nc.tensor.transpose(
                        turned[:, 2 * g + u, :],
                        pairs[:, 256 * g + u : 256 * (g + 1) : 2],
                        ident[:],
                    )
            grouped = stage.tile([P, GROUPS * P * PACK], BF16, align_bytes=64, name="grouped")
            regrouped[index] = grouped
            copy = nc.scalar.copy if index % 2 == 0 else nc.vector.tensor_copy
            copy(
                out=grouped[:].bitcast(F32).rearrange("p (g b u) -> p g b u", g=GROUPS, u=2),
                in_=turned[:].rearrange("p (g u) b -> p g b u", u=2),
            )

        def quantise_tile(index):
            o, m = index // M_TILES, index % M_TILES
            nc.vector.quantize_mx(
                out=a_codes[:, o, m, :].bitcast(FP8X4),
                scales=a_planes[:, o, m, :],
                in_=regrouped[index][:],
            )

        def spread_bias(index):
            gate, half = BIAS_ORDER[index // 2], index % 2
            c0 = gate * WIDTH + half * N_BLOCK
            if half == 0:
                spreads[gate] = psum.tile([P, WIDTH], BF16, tag="bank", name="spread")
            for q in range(N_BLOCK // P):
                row = c0 // P + q
                nc.tensor.matmul(
                    out=spreads[gate][:, half * N_BLOCK + q * P : half * N_BLOCK + (q + 1) * P],
                    lhsT=pick[:, row : row + 1].to_broadcast([P, P]), rhs=bias_rows[:], start=True, stop=True,
                )
            if half == 1:
                nc.scalar.copy(out=bias_all[:, gate * WIDTH : (gate + 1) * WIDTH], in_=spreads[gate][:])

        for index in range(2 * M_TILES):
            if index % 2 == 0:
                spread_bias(index)
                spread_bias(index + 1)
            turn_tile(index)
            if index >= 1:
                quantise_tile(index - 1)
        quantise_tile(2 * M_TILES - 1)

        banks = {}
        gate_tiles = {}

        def multiply(group):
            for bank in group:
                banks[bank] = psum.tile([P, bank[4]], F32, tag="bank", name="acc")
            for kk in range(PASSES):
                for bank in group:
                    one_pass(bank, kk)

        def one_pass(bank, kk):
            if True:
                gate, half, m, first, width = bank
                c0 = gate * WIDTH + half * N_BLOCK + first
                o, g = kk // GROUPS, kk % GROUPS
                nc.tensor.matmul_mx(
                    out=banks[bank][:],
                    lhsT=a_codes[:, o, m, g * P : (g + 1) * P].bitcast(FP8X4),
                    lhsT_scale=a_planes[:, o, m, g * P : (g + 1) * P],
                    rhs=w_words[:, kk, c0 : c0 + width].bitcast(FP8X4),
                    rhs_scale=w_planes[4 * kk : P, o, c0 : c0 + width],
                    start=(kk == 0),
                    stop=(kk == PASSES - 1),
                )

        def leave_psum(bank):
            gate, half, m, first, width = bank
            c0 = gate * WIDTH + half * N_BLOCK + first
            y = work.tile([P, width], F32, tag="gate%d" % gate, name="y")
            gate_tiles[(gate, half, m) if gate != GATE_O else bank] = y
            nc.vector.scalar_tensor_tensor(
                out=y[:], in0=banks[bank][:], scalar=1.0,
                in1=bias_all[:, c0 : c0 + width], op0=ALU.mult, op1=ALU.add,
            )
            if gate != GATE_G:
                nc.scalar.activation(out=y[:], in_=y[:], func=ACT.Relu, bias=0.5, scale=1.0 / 6.0)

        def clip_g(half, m):
            tanh_g = gate_tiles[(GATE_G, half, m)]
            nc.vector.tensor_scalar(out=tanh_g[:], in0=tanh_g[:], scalar1=1.0, scalar2=-1.0, op0=ALU.min, op1=ALU.max)

        def old_part(half, m):
            old = gate_tiles[(GATE_F, half, m)]
            cols = slice(half * N_BLOCK, (half + 1) * N_BLOCK)
            nc.vector.scalar_tensor_tensor(
                out=old[:], in0=old[:], scalar=1.0, in1=c0_sb[:, m, cols], op0=ALU.min, op1=ALU.mult
            )

        def new_part(half, m):
            new = gate_tiles[(GATE_I, half, m)]
            nc.vector.scalar_tensor_tensor(
                out=new[:], in0=new[:], scalar=1.0, in1=gate_tiles[(GATE_G, half, m)][:], op0=ALU.min, op1=ALU.mult
            )

        def sum_cell(half, m):
            rows = slice(m * P, (m + 1) * P)
            cols = slice(half * N_BLOCK, (half + 1) * N_BLOCK)
            new = gate_tiles[(GATE_I, half, m)]
            old = gate_tiles[(GATE_F, half, m)]
            nc.gpsimd.tensor_tensor(out=old[:], in0=old[:], in1=new[:], op=ALU.add)
            nc.sync.dma_start(out=out_1[rows, cols], in_=old[:])
            tanh_c = work.tile([P, N_BLOCK], F32, tag="tanh_c", name="tanh_c")
            gate_tiles[("tanh_c", half, m)] = tanh_c
            nc.gpsimd.tensor_scalar(out=tanh_c[:], in0=old[:], scalar1=1.0, scalar2=-1.0, op0=ALU.min, op1=ALU.max)

        def new_hidden(bank):
            gate, half, m, first, width = bank
            rows = slice(m * P, (m + 1) * P)
            cols = slice(half * N_BLOCK + first, half * N_BLOCK + first + width)
            y = gate_tiles[bank]
            nc.vector.scalar_tensor_tensor(
                out=y[:], in0=y[:], scalar=1.0, in1=gate_tiles[("tanh_c", half, m)][:, first : first + width],
                op0=ALU.min, op1=ALU.mult,
            )
            nc.sync.dma_start(out=out_0[rows, cols], in_=y[:])

        pairs = [(half, first) for half in range(HALVES) for first in range(0, M_TILES, 2)]
        cells = [(half, first + j) for half, first in pairs for j in range(2)]
        first_banks = [(GATE_ORDER[0][0], 0, m, 0, N_BLOCK) for m in range(M_TILES)]
        first_banks += [
            (gate, half, first + j, 0, N_BLOCK)
            for half, first in pairs for gate in GATE_ORDER[half][1 - half :] for j in range(2)
        ]
        last_banks = [(GATE_O, half, m, 0, N_BLOCK) for half in range(HALVES) for m in range(M_TILES)]
        gate, half, m = last_banks.pop()[0:3]
        last_banks += [(gate, half, m, first, LAST_WIDTH) for first in range(0, N_BLOCK, LAST_WIDTH)]
        runs = [first_banks[j : j + RUN] for j in range(0, len(first_banks), RUN)]
        runs += [[bank] for bank in last_banks if bank[4] == N_BLOCK]
        runs.append([bank for bank in last_banks if bank[4] != N_BLOCK])
        follow = {GATE_G: clip_g, GATE_I: new_part, GATE_F: old_part}
        plan = [[] for run in runs]
        for turn, run in enumerate(runs[: len(first_banks) // RUN]):
            for place, bank in enumerate(run):
                late = 1 if (place == RUN - 1 and bank[0] != GATE_G) else 0
                plan[turn + 1 + late].append(bank)
        begun = set()
        ripe = set()
        waiting = []
        multiply(first_banks[0:M_TILES])
        held = []
        summed = []
        for turn, run in enumerate(runs):
            for bank in run:
                if bank not in banks:
                    multiply([bank])
            closing = held
            for bank in plan[turn]:
                if bank[0] != GATE_G and bank[1:3] in begun:
                    closing.append(bank)
                else:
                    follow[bank[0]](*bank[1:3])
                    if bank[0] != GATE_G:
                        begun.add(bank[1:3])
            room = 1 if summed else 2
            held = closing[room:]
            for bank in closing[:room]:
                follow[bank[0]](*bank[1:3])
                sum_cell(*bank[1:3])
                summed.append(bank[1:3])
            for bank in run:
                leave_psum(bank)
            for bank in waiting:
                new_hidden(bank)
            waiting = [bank for bank in run if bank[0] == GATE_O]
        for bank in waiting:
            new_hidden(bank)
